import numpy as np
import ml_dtypes


def mxq(x, axis, fmt="e4m3"):
    dtype, down = {"e4m3": (ml_dtypes.float8_e4m3fn, 7), "e5m2": (ml_dtypes.float8_e5m2, 14)}[fmt]
    v = np.moveaxis(np.asarray(x, np.float32).astype(ml_dtypes.bfloat16).astype(np.float64), axis, -1)
    blocks = v.reshape(v.shape[:-1] + (-1, 32))
    amax = np.abs(blocks).max(-1, keepdims=True)
    byte = np.maximum(np.where(amax > 0, np.frexp(amax)[1] - 1 + 127, 0) - down, 1)
    scale = np.exp2(byte - 127.0)
    codes = (blocks / scale).astype(np.float32).astype(dtype).astype(np.float64)
    return np.moveaxis((codes * scale).reshape(v.shape), -1, axis)


WIDE = False


def mx_kscale(k):
    if not WIDE:
        return np.ones(k)
    levels = np.array([10, -10, 5, -5, 0])
    a = np.random.permutation(np.resize(levels, k // 512 * 4)).reshape(k // 512, 4)
    idx = np.arange(k)
    return np.exp2(a[idx // 512, idx % 128 // 32])


BF16 = ml_dtypes.bfloat16


def bf(x):
    return np.asarray(x, np.float32).astype(BF16)


def f64(x):
    return np.asarray(x).astype(np.float64)


B, N, E, C = 512, 16384, 512, 128
G = 8
R, SIG = 3.0, 0.7


def setup_inputs():
    r = np.maximum(mx_kscale(N), 1.0)
    cen = np.random.standard_normal((G, E)) * R / np.sqrt(E)
    prof = np.exp(np.random.standard_normal((G, C)))
    gx, gk = np.random.randint(G, size=B), np.random.randint(G, size=N)
    x = cen[gx] + np.random.standard_normal((B, E)) * SIG / np.sqrt(E)
    keys = cen[gk] + np.random.standard_normal((N, E)) * SIG / np.sqrt(E)
    values = np.random.uniform(size=(N, C)) * prof[gk] * 0.5 / np.sqrt(N)
    return {"x": bf(x), "keys": bf(keys * r[:, None]), "values": bf(values * (r * r)[:, None])}


def reference(x, keys, values):
    x, keys, values = f64(x), f64(keys), f64(values)
    kn = np.sum(keys * keys, axis=1)[:, None]
    xn = np.sum(x * x, axis=1)[None, :]
    d = kn - 2.0 * (mxq(keys, 1, "e4m3") @ mxq(x, 1, "e4m3").T) + xn
    kern = 1.0 / (d + 1.0)
    KV = mxq(kern, 0, "e4m3").T @ mxq(values, 0, "e4m3")
    return KV / np.sum(KV, axis=1, keepdims=True)

@@ -1,0 +1,382 @@
+from contextlib import ExitStack
+
+import concourse.mybir as mybir
+from concourse.masks import make_identity
+
+F32 = mybir.dt.float32
+BF16 = mybir.dt.bfloat16
+U32 = mybir.dt.uint32
+U8 = mybir.dt.uint8
+FP8X4 = mybir.dt.float8_e4m3fn_x4
+ACT = mybir.ActivationFunctionType
+ALU = mybir.AluOpType
+AX = mybir.AxisListType
+
+P = 128
+B, N, E, C = 512, 16384, 512, 128
+GK = 512
+NG = N // GK
+T = 4
+VCH = 4
+
+G_COLS = 256
+V_COLS = 0
+GRAM_T = 2
+
+FLOPS = 2 * N * B * E + 2 * N * B * C
+
+
+def split(g):
+    late = {NG - 1: (0, 256), NG - 2: (128, 384), NG - 3: (G_COLS, 128)}
+    return late.get(g, (G_COLS, V_COLS))
+
+
+def gram_tiles(g):
+    return GRAM_T if g >= 1 else 0
+
+
+def scalar_banks(g):
+    return 2 if g < 3 else 1
+
+
+def pieces(lo, hi):
+    cuts = []
+    while lo < hi:
+        w = 1
+        while 2 * w <= hi - lo:
+            w = 2 * w
+        cuts.append((lo, lo + w))
+        lo = lo + w
+    return cuts
+
+
+def tile_varkeys_kernel(tc, x, keys, values, out):
+    nc = tc.nc
+    with ExitStack() as ctx:
+        ctx.enter_context(tc.manual_schedule())
+        const = ctx.enter_context(tc.tile_pool(name="const", bufs=1))
+        kin = ctx.enter_context(tc.tile_pool(name="kin", bufs=6))
+        w1 = ctx.enter_context(tc.tile_pool(name="w1", bufs=1))
+        w2 = ctx.enter_context(tc.tile_pool(name="w2", bufs=2))
+        w3 = ctx.enter_context(tc.tile_pool(name="w3", bufs=3))
+        w5 = ctx.enter_context(tc.tile_pool(name="w5", bufs=5))
+        ps_t = ctx.enter_context(tc.psum_pool(name="ps_t", bufs=2))
+        ps_s = ctx.enter_context(tc.psum_pool(name="ps_s", bufs=4))
+        ps_g = ctx.enter_context(tc.psum_pool(name="ps_g", bufs=1))
+        ps_kv = ctx.enter_context(tc.psum_pool(name="ps_kv", bufs=1))
+
+        keys_g = keys.rearrange("(g p t) e -> g p t e", p=P, t=T)
+        vals_g = values.rearrange("(g p t) c -> p g t c", p=P, t=T)
+        st = {}
+
+        def ok(g):
+            return 0 <= g < NG
+
+        def load_keys(g):
+            k_sb = kin.tile([P, T, E], BF16, name="k_sb")
+            nc.sync.dma_start(out=k_sb[:], in_=keys_g[g])
+            st[("k", g)] = k_sb
+
+        v_sb = const.tile([P, NG, T, C], BF16)
+
+        def load_values(j):
+            nc.sync.dma_start(out=v_sb[:, VCH * j : VCH * (j + 1)], in_=vals_g[:, VCH * j : VCH * (j + 1)])
+
+        one = const.tile([P, 1], F32)
+        nc.vector.memset(one[:], 1.0)
+        warm = const.tile([P, 1], F32)
+        nc.scalar.activation(out=warm[:], in_=one[:], func=ACT.Abs_reciprocal_sqrt)
+        ident = const.tile([P, P], F32)
+        make_identity(nc, ident[:])
+
+        x_sb = const.tile([P, 4, E], BF16)
+        nc.sync.dma_start(out=x_sb[:], in_=x.rearrange("(bt p) e -> p bt e", p=P))
+        load_keys(0)
+        load_keys(1)
+        load_keys(2)
+        load_values(0)
+
+        junk = const.tile([P, E], BF16)
+        xn = const.tile([P, 4], F32)
+        for bt in range(4):
+            nc.scalar.activation(out=junk[:], in_=x_sb[:, bt, :], func=ACT.Square, accum_out=xn[:, bt : bt + 1])
+
+        def transposes(src, pool, tag):
+            banks = []
+            for j in range(2):
+                pt = pool.tile([P, 2, 2 * P], F32, name="pt", tag=tag)
+                for tt in range(2):
+                    words = src[:, 2 * j + tt, :].bitcast(F32)
+                    for u in range(2):
+                        nc.tensor.transpose(pt[:, u, P * tt : P * (tt + 1)], words[:, P * u : P * (u + 1)], ident[:])
+                banks.append(pt)
+            return banks
+
+        def copy_out(banks, grouped, j, on_scalar):
+            dst = grouped[:].bitcast(F32).rearrange("p (k u) -> p k u", u=2)[:, 2 * P * j : 2 * P * (j + 1), :]
+            src = banks[j][:].rearrange("p u k -> p k u")
+            if on_scalar:
+                nc.scalar.copy(out=dst, in_=src)
+            else:
+                nc.vector.tensor_copy(out=dst, in_=src)
+
+        xg = const.tile([P, 4 * B], BF16, align_bytes=64)
+        x_banks = transposes(x_sb, ps_s, "s")
+        st[("pt", 0)] = transposes(st[("k", 0)], ps_t, "pt")
+        copy_out(x_banks, xg, 0, False)
+        copy_out(x_banks, xg, 1, False)
+        xc = const.tile([P, B], U32, align_bytes=64)
+        xs = const.tile([P, B], U8, align_bytes=64)
+        xb1 = const.tile([P, B], F32)
+
+        xb_ps = ps_s.tile([P, B], F32, name="xb_ps", tag="s")
+        for bt in range(4):
+            nc.tensor.matmul(
+                out=xb_ps[:, P * bt : P * (bt + 1)],
+                lhsT=xn[:, bt : bt + 1].to_broadcast([P, P]),
+                rhs=ident[:],
+                start=True,
+                stop=True,
+            )
+
+        vc = const.tile([P, NG * C], U32, align_bytes=64)
+        vs = const.tile([P, NG * C], U8, align_bytes=64)
+        kv_ps = ps_kv.tile([P, B], F32)
+
+        nc.vector.quantize_mx(out=xc[:].bitcast(FP8X4), scales=xs[:], in_=xg[:])
+
+        def val_copy(g):
+            vg = w3.tile([P, C, T], BF16, name="vg", align_bytes=64)
+            nc.vector.tensor_copy(
+                out=vg[:].rearrange("p (c i) t -> p c t i", i=4), in_=v_sb[:, g].rearrange("p t (c i) -> p c t i", i=4)
+            )
+            st[("vg", g)] = vg
+
+        def val_quant(g):
+            cols = slice(C * g, C * (g + 1))
+            nc.vector.quantize_mx(
+                out=vc[:, cols].bitcast(FP8X4), scales=vs[:, cols], in_=st[("vg", g)][:].rearrange("p c t -> p (c t)")
+            )
+
+        def tr(g):
+            st[("pt", g)] = transposes(st[("k", g)], ps_t, "pt")
+
+        def tc_alloc(g):
+            st[("kg", g)] = w3.tile([P, 4 * GK], BF16, name="kg", align_bytes=64)
+
+        def tc_v(g):
+            for j in range(2 - scalar_banks(g)):
+                copy_out(st[("pt", g)], st[("kg", g)], j, False)
+
+        def tc_s(g):
+            for j in range(2 - scalar_banks(g), 2):
+                copy_out(st[("pt", g)], st[("kg", g)], j, True)
+
+        def kn_s(g):
+            n_s = T - gram_tiles(g)
+            kn = w5.tile([P, T], F32, name="kn")
+            st[("kn", g)] = kn
+            k_sb = st[("k", g)]
+            for t in range(n_s):
+                nc.scalar.activation(out=junk[:], in_=k_sb[:, t, :], func=ACT.Square, accum_out=kn[:, t : t + 1])
+
+        def gram(g):
+            n_g = gram_tiles(g)
+            if n_g == 0:
+                return
+            kg3 = st[("kg", g)][:].rearrange("p (k j) -> p k j", j=4)
+            gr = ps_g.tile([P, GRAM_T, P], F32, name="gr")
+            for k in range(n_g):
+                t = T - n_g + k
+                for j in range(4):
+                    a = kg3[:, P * t : P * (t + 1), j]
+                    nc.tensor.matmul(out=gr[:, k, :], lhsT=a, rhs=a, start=(j == 0), stop=(j == 3))
+            st[("gr", g)] = gr
+
+        def diag_mask(g):
+            if gram_tiles(g) == 0:
+                return
+            dj = w2.tile([P, GRAM_T, P], F32, name="dj")
+            nc.vector.tensor_tensor(
+                out=dj[:], in0=st[("gr", g)][:], in1=ident[:].unsqueeze(1).to_broadcast([P, GRAM_T, P]), op=ALU.mult
+            )
+            st[("dj", g)] = dj
+
+        def diag_sum(g):
+            if gram_tiles(g) == 0:
+                return
+            kng = w5.tile([P, GRAM_T], F32, name="kng")
+            nc.vector.tensor_reduce(out=kng[:], in_=st[("dj", g)][:], axis=AX.X, op=ALU.add)
+            st[("kng", g)] = kng
+
+        def qk(g):
+            kc = w2.tile([P, GK], U32, name="kc", align_bytes=64)
+            ks = w2.tile([P, GK], U8, name="ks", align_bytes=64)
+            nc.vector.quantize_mx(out=kc[:].bitcast(FP8X4), scales=ks[:], in_=st[("kg", g)][:])
+            st[("kc", g)] = (kc, ks)
+
+        def m1(g, t):
+            kc, ks = st[("kc", g)]
+            s_ps = ps_s.tile([P, B], F32, name="s_ps", tag="s")
+            cols = slice(P * t, P * (t + 1))
+            nc.tensor.matmul_mx(
+                out=s_ps[:],
+                lhsT=kc[:, cols].bitcast(FP8X4),
+                lhsT_scale=ks[:, cols],
+                rhs=xc[:].bitcast(FP8X4),
+                rhs_scale=xs[:],
+                start=True,
+                stop=True,
+            )
+            st[("s", g, t)] = s_ps
+
+        def stt(g, t):
+            if t == 0:
+                st[("y", g)] = w3.tile([P, T, B], F32, name="y")
+            nc.vector.scalar_tensor_tensor(
+                out=st[("y", g)][:, t, :], in0=st[("s", g, t)][:], scalar=-2.0, in1=xb1[:], op0=ALU.mult, op1=ALU.add
+            )
+
+        def rs(g, t):
+            if t == 0:
+                st[("r", g)] = w3.tile([P, T, B], F32, name="r")
+            n_s = T - gram_tiles(g)
+            if t < n_s:
+                bias = st[("kn", g)][:, t : t + 1]
+            else:
+                bias = st[("kng", g)][:, t - n_s : t - n_s + 1]
+            nc.scalar.activation(
+                out=st[("r", g)][:, t, :], in_=st[("y", g)][:, t, :], func=ACT.Abs_reciprocal_sqrt, bias=bias, scale=1.0
+            )
+
+        def sq_views(kb, base, g, lo, hi):
+            r = st[("r", g)]
+            return (
+                kb[:, lo - base : hi - base, :].rearrange("p (c i) t -> p c t i", i=4),
+                r[:, :, lo:hi].rearrange("p t (c i) -> p c t i", i=4),
+            )
+
+        def sq_alloc_s(g):
+            st[("kbs", g)] = w2.tile([P, B - split(g)[0], T], BF16, name="kbs", tag="kbs", align_bytes=64)
+
+        def sq_g(g):
+            gc = split(g)[0]
+            if gc == 0:
+                return
+            kbg = w1.tile([P, gc, T], BF16, name="kbg", tag="kbg", align_bytes=64)
+            st[("kbg", g)] = kbg
+            o, i = sq_views(kbg, 0, g, 0, gc)
+            nc.gpsimd.tensor_tensor(out=o, in0=i, in1=i, op=ALU.mult)
+
+        def sq_v(g):
+            gc, vcols = split(g)
+            if vcols == 0:
+                return
+            o, i = sq_views(st[("kbs", g)], gc, g, gc, gc + vcols)
+            nc.vector.tensor_tensor(out=o, in0=i, in1=i, op=ALU.mult)
+
+        def sq_s(g):
+            gc, vcols = split(g)
+            if gc + vcols >= B:
+                return
+            o, i = sq_views(st[("kbs", g)], gc, g, gc + vcols, B)
+            nc.scalar.activation(out=o, in_=i, func=ACT.Square)
+
+        def qp_part(g, kb, base, lo, hi):
+            qc, qs = st[("qc", g)]
+            for a, b in pieces(lo, hi):
+                nc.vector.quantize_mx(
+                    out=qc[:, a:b].bitcast(FP8X4),
+                    scales=qs[:, a:b],
+                    in_=kb[:, a - base : b - base, :].rearrange("p b t -> p (b t)"),
+                )
+
+        def qp_s(g):
+            qc = w2.tile([P, B], U32, name="qc", align_bytes=64)
+            qs = w2.tile([P, B], U8, name="qs", align_bytes=64)
+            st[("qc", g)] = (qc, qs)
+            gc = split(g)[0]
+            qp_part(g, st[("kbs", g)], gc, gc, B)
+
+        def qp_g(g):
+            gc = split(g)[0]
+            if gc:
+                qp_part(g, st[("kbg", g)], 0, 0, gc)
+
+        def m2(g):
+            qc, qs = st[("qc", g)]
+            cols = slice(C * g, C * (g + 1))
+            nc.tensor.matmul_mx(
+                out=kv_ps[:],
+                lhsT=vc[:, cols].bitcast(FP8X4),
+                lhsT_scale=vs[:, cols],
+                rhs=qc[:].bitcast(FP8X4),
+                rhs_scale=qs[:],
+                start=(g == 0),
+                stop=(g == NG - 1),
+            )
+
+        for i in range(-2, NG + 3):
+            if ok(i + 5) and i + 5 > 2:
+                load_keys(i + 5)
+            if (i + 2) % VCH == 0 and (i + 2) // VCH + 1 < NG // VCH:
+                load_values((i + 2) // VCH + 1)
+            if ok(i):
+                val_copy(i)
+            if ok(i + 1):
+                qk(i + 1)
+            if ok(i - 1):
+                val_quant(i - 1)
+            if ok(i - 3):
+                qp_s(i - 3)
+            if ok(i - 2):
+                sq_alloc_s(i - 2)
+                sq_v(i - 2)
+            if ok(i - 3):
+                qp_g(i - 3)
+            if ok(i - 2):
+                sq_g(i - 2)
+            if i == -1:
+                nc.vector.tensor_scalar_add(out=xb1[:], in0=xb_ps[:], scalar1=1.0)
+                for t in range(T):
+                    m1(0, t)
+            if ok(i + 1):
+                gram(i + 1)
+            if ok(i + 2):
+                tc_alloc(i + 2)
+                tc_v(i + 2)
+            if ok(i + 2):
+                tc_s(i + 2)
+            if ok(i - 1):
+                for t in range(T):
+                    rs(i - 1, t)
+            if ok(i + 3):
+                tr(i + 3)
+            if ok(i + 1) and i != -1:
+                for t in range(T):
+                    m1(i + 1, t)
+            if ok(i - 3):
+                m2(i - 3)
+            if ok(i):
+                diag_sum(i)
+                for t in range(T):
+                    stt(i, t)
+            if ok(i + 1):
+                diag_mask(i + 1)
+            if ok(i + 2):
+                kn_s(i + 2)
+            if ok(i - 2):
+                sq_s(i - 2)
+
+        kv_sb = const.tile([P, B], F32)
+        nc.scalar.copy(out=kv_sb[:], in_=kv_ps[:])
+        o_ps = ps_t.tile([P, 4, C], F32, name="o_ps", tag="pt")
+        for bt in range(4):
+            nc.tensor.transpose(o_ps[:, bt, :], kv_sb[:, P * bt : P * (bt + 1)], ident[:])
+        rsum = const.tile([P, 4], F32)
+        nc.vector.tensor_reduce(out=rsum[:], in_=o_ps[:], axis=AX.X, op=ALU.add)
+        rinv = const.tile([P, 4], F32)
+        nc.vector.reciprocal(out=rinv[:], in_=rsum[:])
+        o_sb = const.tile([P, 4, C], F32)
+        nc.vector.tensor_tensor(out=o_sb[:], in0=o_ps[:], in1=rinv[:].unsqueeze(2).to_broadcast([P, 4, C]), op=ALU.mult)
+        nc.sync.dma_start(out=out.rearrange("(bt p) c -> p bt c", p=P), in_=o_sb[:])

@@ -36,7 +36,7 @@ def gram_tiles(g):
 
 
 def scalar_banks(g):
-    return 2 if g < 3 else 1
+    return 2 if g < 3 else g % 2
 
 
 def pieces(lo, hi):
@@ -147,8 +147,13 @@ def tile_varkeys_kernel(tc, x, keys, values, out):
 
         def val_copy(g):
             vg = w3.tile([P, C, T], BF16, name="vg", align_bytes=64)
-            nc.vector.tensor_copy(
-                out=vg[:].rearrange("p (c i) t -> p c t i", i=4), in_=v_sb[:, g].rearrange("p t (c i) -> p c t i", i=4)
+            nc.gpsimd.tensor_scalar(
+                out=vg[:].rearrange("p (c i) t -> p c t i", i=4),
+                in0=v_sb[:, g].rearrange("p t (c i) -> p c t i", i=4),
+                scalar1=1.0,
+                scalar2=0.0,
+                op0=ALU.mult,
+                op1=ALU.add,
             )
             st[("vg", g)] = vg
 
@@ -193,20 +198,22 @@ def tile_varkeys_kernel(tc, x, keys, values, out):
                     nc.tensor.matmul(out=gr[:, k, :], lhsT=a, rhs=a, start=(j == 0), stop=(j == 3))
             st[("gr", g)] = gr
 
-        def diag_mask(g):
-            if gram_tiles(g) == 0:
-                return
-            dj = w2.tile([P, GRAM_T, P], F32, name="dj")
-            nc.vector.tensor_tensor(
-                out=dj[:], in0=st[("gr", g)][:], in1=ident[:].unsqueeze(1).to_broadcast([P, GRAM_T, P]), op=ALU.mult
-            )
-            st[("dj", g)] = dj
-
-        def diag_sum(g):
-            if gram_tiles(g) == 0:
+        def diag(g):
+            n_g = gram_tiles(g)
+            if n_g == 0:
                 return
             kng = w5.tile([P, GRAM_T], F32, name="kng")
-            nc.vector.tensor_reduce(out=kng[:], in_=st[("dj", g)][:], axis=AX.X, op=ALU.add)
+            for k in range(n_g):
+                dj = w2.tile([P, P], F32, name="dj")
+                nc.vector.scalar_tensor_tensor(
+                    out=dj[:],
+                    in0=st[("gr", g)][:, k, :],
+                    scalar=1.0,
+                    in1=ident[:],
+                    op0=ALU.mult,
+                    op1=ALU.mult,
+                    accum_out=kng[:, k : k + 1],
+                )
             st[("kng", g)] = kng
 
         def qk(g):
@@ -321,8 +328,6 @@ def tile_varkeys_kernel(tc, x, keys, values, out):
                 load_keys(i + 5)
             if (i + 2) % VCH == 0 and (i + 2) // VCH + 1 < NG // VCH:
                 load_values((i + 2) // VCH + 1)
-            if ok(i):
-                val_copy(i)
             if ok(i + 1):
                 qk(i + 1)
             if ok(i - 1):
@@ -336,6 +341,8 @@ def tile_varkeys_kernel(tc, x, keys, values, out):
                 qp_g(i - 3)
             if ok(i - 2):
                 sq_g(i - 2)
+            if ok(i):
+                val_copy(i)
             if i == -1:
                 nc.vector.tensor_scalar_add(out=xb1[:], in0=xb_ps[:], scalar1=1.0)
                 for t in range(T):
@@ -358,11 +365,10 @@ def tile_varkeys_kernel(tc, x, keys, values, out):
             if ok(i - 3):
                 m2(i - 3)
             if ok(i):
-                diag_sum(i)
                 for t in range(T):
                     stt(i, t)
             if ok(i + 1):
-                diag_mask(i + 1)
+                diag(i + 1)
             if ok(i + 2):
                 kn_s(i + 2)
             if ok(i - 2):

@@ -256,11 +256,11 @@ def tile_varkeys_kernel(tc, x, keys, values, out):
                 out=st[("r", g)][:, t, :], in_=st[("y", g)][:, t, :], func=ACT.Abs_reciprocal_sqrt, bias=bias, scale=1.0
             )
 
-        def sq_views(kb, base, g, lo, hi):
+        def sq_views(kb, base, g, lo, hi, run):
             r = st[("r", g)]
             return (
-                kb[:, lo - base : hi - base, :].rearrange("p (c i) t -> p c t i", i=4),
-                r[:, :, lo:hi].rearrange("p t (c i) -> p c t i", i=4),
+                kb[:, lo - base : hi - base, :].rearrange("p (c i) t -> p c t i", i=run),
+                r[:, :, lo:hi].rearrange("p t (c i) -> p c t i", i=run),
             )
 
         def sq_alloc_s(g):
@@ -272,21 +272,21 @@ def tile_varkeys_kernel(tc, x, keys, values, out):
                 return
             kbg = w1.tile([P, gc, T], BF16, name="kbg", tag="kbg", align_bytes=64)
             st[("kbg", g)] = kbg
-            o, i = sq_views(kbg, 0, g, 0, gc)
+            o, i = sq_views(kbg, 0, g, 0, gc, 4)
             nc.gpsimd.tensor_tensor(out=o, in0=i, in1=i, op=ALU.mult)
 
         def sq_v(g):
             gc, vcols = split(g)
             if vcols == 0:
                 return
-            o, i = sq_views(st[("kbs", g)], gc, g, gc, gc + vcols)
+            o, i = sq_views(st[("kbs", g)], gc, g, gc, gc + vcols, 4)
             nc.vector.tensor_tensor(out=o, in0=i, in1=i, op=ALU.mult)
 
         def sq_s(g):
             gc, vcols = split(g)
             if gc + vcols >= B:
                 return
-            o, i = sq_views(st[("kbs", g)], gc, g, gc + vcols, B)
+            o, i = sq_views(st[("kbs", g)], gc, g, gc + vcols, B, 2)
             nc.scalar.activation(out=o, in_=i, func=ACT.Square)
 
         def qp_part(g, kb, base, lo, hi):

@@ -148,8 +148,8 @@ def tile_varkeys_kernel(tc, x, keys, values, out):
         def val_copy(g):
             vg = w3.tile([P, C, T], BF16, name="vg", align_bytes=64)
             nc.gpsimd.tensor_scalar(
-                out=vg[:].rearrange("p (c i) t -> p c t i", i=4),
-                in0=v_sb[:, g].rearrange("p t (c i) -> p c t i", i=4),
+                out=vg[:],
+                in0=v_sb[:, g].rearrange("p t c -> p c t"),
                 scalar1=1.0,
                 scalar2=0.0,
                 op0=ALU.mult,
@@ -272,7 +272,7 @@ def tile_varkeys_kernel(tc, x, keys, values, out):
                 return
             kbg = w1.tile([P, gc, T], BF16, name="kbg", tag="kbg", align_bytes=64)
             st[("kbg", g)] = kbg
-            o, i = sq_views(kbg, 0, g, 0, gc, 4)
+            o, i = sq_views(kbg, 0, g, 0, gc, 1)
             nc.gpsimd.tensor_tensor(out=o, in0=i, in1=i, op=ALU.mult)
 
         def sq_v(g):

@@ -22,6 +22,9 @@ VCH = 4
 G_COLS = 256
 V_COLS = 0
 GRAM_T = 2
+XN_V = 2
+GRAM_0 = 1
+KB_BUFS = 2
 
 FLOPS = 2 * N * B * E + 2 * N * B * C
 
@@ -32,22 +35,11 @@ def split(g):
 
 
 def gram_tiles(g):
-    return GRAM_T if g >= 1 else 0
+    return GRAM_T if g >= 1 else GRAM_0
 
 
 def scalar_banks(g):
-    return 2 if g < 3 else g % 2
-
-
-def pieces(lo, hi):
-    cuts = []
-    while lo < hi:
-        w = 1
-        while 2 * w <= hi - lo:
-            w = 2 * w
-        cuts.append((lo, lo + w))
-        lo = lo + w
-    return cuts
+    return 1 if g < 3 else g % 2
 
 
 def tile_varkeys_kernel(tc, x, keys, values, out):
@@ -56,7 +48,7 @@ def tile_varkeys_kernel(tc, x, keys, values, out):
         ctx.enter_context(tc.manual_schedule())
         const = ctx.enter_context(tc.tile_pool(name="const", bufs=1))
         kin = ctx.enter_context(tc.tile_pool(name="kin", bufs=6))
-        w1 = ctx.enter_context(tc.tile_pool(name="w1", bufs=1))
+        kbp = ctx.enter_context(tc.tile_pool(name="kbp", bufs=KB_BUFS))
         w2 = ctx.enter_context(tc.tile_pool(name="w2", bufs=2))
         w3 = ctx.enter_context(tc.tile_pool(name="w3", bufs=3))
         w5 = ctx.enter_context(tc.tile_pool(name="w5", bufs=5))
@@ -98,8 +90,20 @@ def tile_varkeys_kernel(tc, x, keys, values, out):
 
         junk = const.tile([P, E], BF16)
         xn = const.tile([P, 4], F32)
+        junk_v = const.tile([P, E], F32)
         for bt in range(4):
-            nc.scalar.activation(out=junk[:], in_=x_sb[:, bt, :], func=ACT.Square, accum_out=xn[:, bt : bt + 1])
+            if bt < XN_V:
+                nc.vector.scalar_tensor_tensor(
+                    out=junk_v[:],
+                    in0=x_sb[:, bt, :],
+                    scalar=1.0,
+                    in1=x_sb[:, bt, :],
+                    op0=ALU.mult,
+                    op1=ALU.mult,
+                    accum_out=xn[:, bt : bt + 1],
+                )
+            else:
+                nc.scalar.activation(out=junk[:], in_=x_sb[:, bt, :], func=ACT.Square, accum_out=xn[:, bt : bt + 1])
 
         def transposes(src, pool, tag):
             banks = []
@@ -131,13 +135,7 @@ def tile_varkeys_kernel(tc, x, keys, values, out):
 
         xb_ps = ps_s.tile([P, B], F32, name="xb_ps", tag="s")
         for bt in range(4):
-            nc.tensor.matmul(
-                out=xb_ps[:, P * bt : P * (bt + 1)],
-                lhsT=xn[:, bt : bt + 1].to_broadcast([P, P]),
-                rhs=ident[:],
-                start=True,
-                stop=True,
-            )
+            nc.tensor.transpose(xb_ps[:, P * bt : P * (bt + 1)], xn[:, bt : bt + 1].to_broadcast([P, P]), ident[:])
 
         vc = const.tile([P, NG * C], U32, align_bytes=64)
         vs = const.tile([P, NG * C], U8, align_bytes=64)
@@ -256,59 +254,43 @@ def tile_varkeys_kernel(tc, x, keys, values, out):
                 out=st[("r", g)][:, t, :], in_=st[("y", g)][:, t, :], func=ACT.Abs_reciprocal_sqrt, bias=bias, scale=1.0
             )
 
-        def sq_views(kb, base, g, lo, hi, run):
-            r = st[("r", g)]
+        def sq_views(g, lo, hi, run):
             return (
-                kb[:, lo - base : hi - base, :].rearrange("p (c i) t -> p c t i", i=run),
-                r[:, :, lo:hi].rearrange("p t (c i) -> p c t i", i=run),
+                st[("kb", g)][:, lo:hi, :].rearrange("p (c i) t -> p c t i", i=run),
+                st[("r", g)][:, :, lo:hi].rearrange("p t (c i) -> p c t i", i=run),
             )
 
-        def sq_alloc_s(g):
-            st[("kbs", g)] = w2.tile([P, B - split(g)[0], T], BF16, name="kbs", tag="kbs", align_bytes=64)
+        def sq_alloc(g):
+            st[("kb", g)] = kbp.tile([P, B, T], BF16, name="kb", tag="kb", align_bytes=64)
 
         def sq_g(g):
             gc = split(g)[0]
             if gc == 0:
                 return
-            kbg = w1.tile([P, gc, T], BF16, name="kbg", tag="kbg", align_bytes=64)
-            st[("kbg", g)] = kbg
-            o, i = sq_views(kbg, 0, g, 0, gc, 1)
+            o, i = sq_views(g, 0, gc, 1)
             nc.gpsimd.tensor_tensor(out=o, in0=i, in1=i, op=ALU.mult)
 
         def sq_v(g):
             gc, vcols = split(g)
             if vcols == 0:
                 return
-            o, i = sq_views(st[("kbs", g)], gc, g, gc, gc + vcols, 4)
+            o, i = sq_views(g, gc, gc + vcols, 4)
             nc.vector.tensor_tensor(out=o, in0=i, in1=i, op=ALU.mult)
 
         def sq_s(g):
             gc, vcols = split(g)
             if gc + vcols >= B:
                 return
-            o, i = sq_views(st[("kbs", g)], gc, g, gc + vcols, B, 2)
+            o, i = sq_views(g, gc + vcols, B, 2)
             nc.scalar.activation(out=o, in_=i, func=ACT.Square)
 
-        def qp_part(g, kb, base, lo, hi):
-            qc, qs = st[("qc", g)]
-            for a, b in pieces(lo, hi):
-                nc.vector.quantize_mx(
-                    out=qc[:, a:b].bitcast(FP8X4),
-                    scales=qs[:, a:b],
-                    in_=kb[:, a - base : b - base, :].rearrange("p b t -> p (b t)"),
-                )
-
-        def qp_s(g):
+        def qp(g):
             qc = w2.tile([P, B], U32, name="qc", align_bytes=64)
             qs = w2.tile([P, B], U8, name="qs", align_bytes=64)
             st[("qc", g)] = (qc, qs)
-            gc = split(g)[0]
-            qp_part(g, st[("kbs", g)], gc, gc, B)
-
-        def qp_g(g):
-            gc = split(g)[0]
-            if gc:
-                qp_part(g, st[("kbg", g)], 0, 0, gc)
+            nc.vector.quantize_mx(
+                out=qc[:].bitcast(FP8X4), scales=qs[:], in_=st[("kb", g)][:].rearrange("p b t -> p (b t)")
+            )
 
         def m2(g):
             qc, qs = st[("qc", g)]
@@ -333,13 +315,10 @@ def tile_varkeys_kernel(tc, x, keys, values, out):
             if ok(i - 1):
                 val_quant(i - 1)
             if ok(i - 3):
-                qp_s(i - 3)
+                qp(i - 3)
             if ok(i - 2):
-                sq_alloc_s(i - 2)
+                sq_alloc(i - 2)
                 sq_v(i - 2)
-            if ok(i - 3):
-                qp_g(i - 3)
-            if ok(i - 2):
                 sq_g(i - 2)
             if ok(i):
                 val_copy(i)
@@ -374,15 +353,33 @@ def tile_varkeys_kernel(tc, x, keys, values, out):
             if ok(i - 2):
                 sq_s(i - 2)
 
+        ones = const.tile([P, 1], F32)
+        nc.gpsimd.memset(ones[:], 1.0)
         kv_sb = const.tile([P, B], F32)
-        nc.scalar.copy(out=kv_sb[:], in_=kv_ps[:])
-        o_ps = ps_t.tile([P, 4, C], F32, name="o_ps", tag="pt")
-        for bt in range(4):
-            nc.tensor.transpose(o_ps[:, bt, :], kv_sb[:, P * bt : P * (bt + 1)], ident[:])
-        rsum = const.tile([P, 4], F32)
-        nc.vector.tensor_reduce(out=rsum[:], in_=o_ps[:], axis=AX.X, op=ALU.add)
+        sum_ps = ps_g.tile([P, 4], F32, name="sum_ps", tag="gr")
+        o_ps = []
+        for h in range(2):
+            cols = slice(2 * P * h, 2 * P * (h + 1))
+            nc.scalar.copy(out=kv_sb[:, cols], in_=kv_ps[:, cols])
+        for h in range(2):
+            o_half = ps_t.tile([P, 2, C], F32, name="o_half", tag="pt")
+            for k in range(2):
+                rows = kv_sb[:, P * (2 * h + k) : P * (2 * h + k + 1)]
+                nc.tensor.matmul(
+                    out=sum_ps[:, 2 * h + k : 2 * h + k + 1], lhsT=rows, rhs=ones[:], start=True, stop=True
+                )
+                nc.tensor.transpose(o_half[:, k, :], rows, ident[:])
+            o_ps.append(o_half)
         rinv = const.tile([P, 4], F32)
-        nc.vector.reciprocal(out=rinv[:], in_=rsum[:])
+        nc.vector.reciprocal(out=rinv[:], in_=sum_ps[:])
         o_sb = const.tile([P, 4, C], F32)
-        nc.vector.tensor_tensor(out=o_sb[:], in0=o_ps[:], in1=rinv[:].unsqueeze(2).to_broadcast([P, 4, C]), op=ALU.mult)
-        nc.sync.dma_start(out=out.rearrange("(bt p) c -> p bt c", p=P), in_=o_sb[:])
+        out_v = out.rearrange("(bt p) c -> p bt c", p=P)
+        nc.vector.tensor_tensor(
+            out=o_sb[:, 0:2, :], in0=o_ps[0][:], in1=rinv[:, 0:2].unsqueeze(2).to_broadcast([P, 2, C]), op=ALU.mult
+        )
+        nc.sync.dma_start(out=out_v[:, 0:2, :], in_=o_sb[:, 0:2, :])
+        for k in range(2):
+            nc.scalar.activation(
+                out=o_sb[:, 2 + k, :], in_=o_ps[1][:, k, :], func=ACT.Copy, scale=rinv[:, 2 + k : 3 + k]
+            )
+        nc.scalar.dma_start(out=out_v[:, 2:4, :], in_=o_sb[:, 2:4, :])

@@ -22,15 +22,18 @@ VCH = 4
 G_COLS = 256
 V_COLS = 0
 GRAM_T = 2
-XN_V = 2
+XN_V = 0
+RS_T = 2
+RS_LAST = 1
 GRAM_0 = 1
 KB_BUFS = 2
+SQ_I = NG
 
 FLOPS = 2 * N * B * E + 2 * N * B * C
 
 
 def split(g):
-    late = {NG - 1: (0, 256), NG - 2: (128, 384), NG - 3: (G_COLS, 128)}
+    late = {NG - 1: (0, 256), NG - 2: (G_COLS, 0), NG - 3: (G_COLS, 128)}
     return late.get(g, (G_COLS, V_COLS))
 
 
@@ -88,6 +91,9 @@ def tile_varkeys_kernel(tc, x, keys, values, out):
         load_keys(2)
         load_values(0)
 
+        x_m2 = const.tile([P, 4, E], BF16)
+        nc.vector.tensor_scalar_mul(out=x_m2[:], in0=x_sb[:], scalar1=-2.0)
+
         junk = const.tile([P, E], BF16)
         xn = const.tile([P, 4], F32)
         junk_v = const.tile([P, E], F32)
@@ -125,7 +131,7 @@ def tile_varkeys_kernel(tc, x, keys, values, out):
                 nc.vector.tensor_copy(out=dst, in_=src)
 
         xg = const.tile([P, 4 * B], BF16, align_bytes=64)
-        x_banks = transposes(x_sb, ps_s, "s")
+        x_banks = transposes(x_m2, ps_s, "s")
         st[("pt", 0)] = transposes(st[("k", 0)], ps_t, "pt")
         copy_out(x_banks, xg, 0, False)
         copy_out(x_banks, xg, 1, False)
@@ -238,21 +244,24 @@ def tile_varkeys_kernel(tc, x, keys, values, out):
         def stt(g, t):
             if t == 0:
                 st[("y", g)] = w3.tile([P, T, B], F32, name="y")
-            nc.vector.scalar_tensor_tensor(
-                out=st[("y", g)][:, t, :], in0=st[("s", g, t)][:], scalar=-2.0, in1=xb1[:], op0=ALU.mult, op1=ALU.add
-            )
-
-        def rs(g, t):
-            if t == 0:
-                st[("r", g)] = w3.tile([P, T, B], F32, name="r")
             n_s = T - gram_tiles(g)
             if t < n_s:
-                bias = st[("kn", g)][:, t : t + 1]
+                kn_t = st[("kn", g)][:, t : t + 1]
             else:
-                bias = st[("kng", g)][:, t - n_s : t - n_s + 1]
-            nc.scalar.activation(
-                out=st[("r", g)][:, t, :], in_=st[("y", g)][:, t, :], func=ACT.Abs_reciprocal_sqrt, bias=bias, scale=1.0
+                kn_t = st[("kng", g)][:, t - n_s : t - n_s + 1]
+            nc.vector.scalar_tensor_tensor(
+                out=st[("y", g)][:, t, :], in0=st[("s", g, t)][:], scalar=kn_t, in1=xb1[:], op0=ALU.add, op1=ALU.add
             )
+
+        def rs(g):
+            st[("r", g)] = w3.tile([P, T, B], F32, name="r")
+            step = RS_LAST if g == NG - 1 else RS_T
+            for t in range(0, T, step):
+                nc.scalar.activation(
+                    out=st[("r", g)][:, t : t + step, :],
+                    in_=st[("y", g)][:, t : t + step, :],
+                    func=ACT.Abs_reciprocal_sqrt,
+                )
 
         def sq_views(g, lo, hi, run):
             return (
@@ -320,8 +329,8 @@ def tile_varkeys_kernel(tc, x, keys, values, out):
                 sq_alloc(i - 2)
                 sq_v(i - 2)
                 sq_g(i - 2)
-            if ok(i):
-                val_copy(i)
+            if ok(i + 1):
+                val_copy(i + 1)
             if i == -1:
                 nc.vector.tensor_scalar_add(out=xb1[:], in0=xb_ps[:], scalar1=1.0)
                 for t in range(T):
@@ -333,9 +342,10 @@ def tile_varkeys_kernel(tc, x, keys, values, out):
                 tc_v(i + 2)
             if ok(i + 2):
                 tc_s(i + 2)
+            if ok(i - 2) and i >= SQ_I:
+                sq_s(i - 2)
             if ok(i - 1):
-                for t in range(T):
-                    rs(i - 1, t)
+                rs(i - 1)
             if ok(i + 3):
                 tr(i + 3)
             if ok(i + 1) and i != -1:
@@ -350,7 +360,7 @@ def tile_varkeys_kernel(tc, x, keys, values, out):
                 diag(i + 1)
             if ok(i + 2):
                 kn_s(i + 2)
-            if ok(i - 2):
+            if ok(i - 2) and i < SQ_I:
                 sq_s(i - 2)
 
         ones = const.tile([P, 1], F32)

@@ -18,6 +18,7 @@ GK = 512
 NG = N // GK
 T = 4
 VCH = 4
+TILE_ORDER = (0, 1, 3, 2)
 
 G_COLS = 256
 V_COLS = 0
@@ -85,14 +86,17 @@ def tile_varkeys_kernel(tc, x, keys, values, out):
         make_identity(nc, ident[:])
 
         x_sb = const.tile([P, 4, E], BF16)
-        nc.sync.dma_start(out=x_sb[:], in_=x.rearrange("(bt p) e -> p bt e", p=P))
+        x_v = x.rearrange("(bt p) e -> p bt e", p=P)
+        for bt in range(4):
+            nc.sync.dma_start(out=x_sb[:, bt, :], in_=x_v[:, bt, :])
         load_keys(0)
         load_keys(1)
         load_keys(2)
         load_values(0)
 
         x_m2 = const.tile([P, 4, E], BF16)
-        nc.vector.tensor_scalar_mul(out=x_m2[:], in0=x_sb[:], scalar1=-2.0)
+        for bt in range(4):
+            nc.vector.tensor_scalar_mul(out=x_m2[:, bt, :], in0=x_sb[:, bt, :], scalar1=-2.0)
 
         junk = const.tile([P, E], BF16)
         xn = const.tile([P, 4], F32)
@@ -242,7 +246,7 @@ def tile_varkeys_kernel(tc, x, keys, values, out):
             st[("s", g, t)] = s_ps
 
         def stt(g, t):
-            if t == 0:
+            if t == TILE_ORDER[0]:
                 st[("y", g)] = w3.tile([P, T, B], F32, name="y")
             n_s = T - gram_tiles(g)
             if t < n_s:
@@ -321,8 +325,8 @@ def tile_varkeys_kernel(tc, x, keys, values, out):
                 load_values((i + 2) // VCH + 1)
             if ok(i + 1):
                 qk(i + 1)
-            if ok(i - 1):
-                val_quant(i - 1)
+            if ok(i):
+                val_quant(i)
             if ok(i - 3):
                 qp(i - 3)
             if ok(i - 2):
@@ -333,7 +337,7 @@ def tile_varkeys_kernel(tc, x, keys, values, out):
                 val_copy(i + 1)
             if i == -1:
                 nc.vector.tensor_scalar_add(out=xb1[:], in0=xb_ps[:], scalar1=1.0)
-                for t in range(T):
+                for t in TILE_ORDER:
                     m1(0, t)
             if ok(i + 1):
                 gram(i + 1)
@@ -349,12 +353,12 @@ def tile_varkeys_kernel(tc, x, keys, values, out):
             if ok(i + 3):
                 tr(i + 3)
             if ok(i + 1) and i != -1:
-                for t in range(T):
+                for t in TILE_ORDER:
                     m1(i + 1, t)
             if ok(i - 3):
                 m2(i - 3)
             if ok(i):
-                for t in range(T):
+                for t in TILE_ORDER:
                     stt(i, t)
             if ok(i + 1):
                 diag(i + 1)
@@ -363,25 +367,21 @@ def tile_varkeys_kernel(tc, x, keys, values, out):
             if ok(i - 2) and i < SQ_I:
                 sq_s(i - 2)
 
-        ones = const.tile([P, 1], F32)
-        nc.gpsimd.memset(ones[:], 1.0)
         kv_sb = const.tile([P, B], F32)
-        sum_ps = ps_g.tile([P, 4], F32, name="sum_ps", tag="gr")
-        o_ps = []
         for h in range(2):
             cols = slice(2 * P * h, 2 * P * (h + 1))
             nc.scalar.copy(out=kv_sb[:, cols], in_=kv_ps[:, cols])
+        rsum = const.tile([P, 4], F32)
+        o_ps = []
         for h in range(2):
             o_half = ps_t.tile([P, 2, C], F32, name="o_half", tag="pt")
             for k in range(2):
-                rows = kv_sb[:, P * (2 * h + k) : P * (2 * h + k + 1)]
-                nc.tensor.matmul(
-                    out=sum_ps[:, 2 * h + k : 2 * h + k + 1], lhsT=rows, rhs=ones[:], start=True, stop=True
-                )
-                nc.tensor.transpose(o_half[:, k, :], rows, ident[:])
+                bt = 2 * h + k
+                nc.tensor.transpose(o_half[:, k, :], kv_sb[:, P * bt : P * (bt + 1)], ident[:])
+            nc.vector.tensor_reduce(out=rsum[:, 2 * h : 2 * (h + 1)], in_=o_half[:], axis=AX.X, op=ALU.add)
             o_ps.append(o_half)
         rinv = const.tile([P, 4], F32)
-        nc.vector.reciprocal(out=rinv[:], in_=sum_ps[:])
+        nc.vector.reciprocal(out=rinv[:], in_=rsum[:])
         o_sb = const.tile([P, 4, C], F32)
         out_v = out.rearrange("(bt p) c -> p bt c", p=P)
         nc.vector.tensor_tensor(

@@ -20,14 +20,14 @@ T = 4
 VCH = 4
 TILE_ORDER = (0, 1, 3, 2)
 
-G_COLS = 256
+G_COLS = 272
 V_COLS = 0
 GRAM_T = 2
 XN_V = 0
 RS_T = 2
 RS_LAST = 1
 GRAM_0 = 1
-KB_BUFS = 2
+KB_BUFS = 3
 SQ_I = NG
 
 FLOPS = 2 * N * B * E + 2 * N * B * C
@@ -324,6 +324,10 @@ def tile_varkeys_kernel(tc, x, keys, values, out):
             if (i + 2) % VCH == 0 and (i + 2) // VCH + 1 < NG // VCH:
                 load_values((i + 2) // VCH + 1)
             if ok(i + 1):
+                gram(i + 1)
+            if ok(i + 3):
+                tr(i + 3)
+            if ok(i + 1):
                 qk(i + 1)
             if ok(i):
                 val_quant(i)
@@ -337,22 +341,10 @@ def tile_varkeys_kernel(tc, x, keys, values, out):
                 val_copy(i + 1)
             if i == -1:
                 nc.vector.tensor_scalar_add(out=xb1[:], in0=xb_ps[:], scalar1=1.0)
-                for t in TILE_ORDER:
-                    m1(0, t)
-            if ok(i + 1):
-                gram(i + 1)
             if ok(i + 2):
                 tc_alloc(i + 2)
                 tc_v(i + 2)
-            if ok(i + 2):
-                tc_s(i + 2)
-            if ok(i - 2) and i >= SQ_I:
-                sq_s(i - 2)
-            if ok(i - 1):
-                rs(i - 1)
-            if ok(i + 3):
-                tr(i + 3)
-            if ok(i + 1) and i != -1:
+            if ok(i + 1):
                 for t in TILE_ORDER:
                     m1(i + 1, t)
             if ok(i - 3):
@@ -362,10 +354,16 @@ def tile_varkeys_kernel(tc, x, keys, values, out):
                     stt(i, t)
             if ok(i + 1):
                 diag(i + 1)
-            if ok(i + 2):
-                kn_s(i + 2)
+            if ok(i - 2) and i >= SQ_I:
+                sq_s(i - 2)
+            if ok(i - 1):
+                rs(i - 1)
             if ok(i - 2) and i < SQ_I:
                 sq_s(i - 2)
+            if ok(i + 2):
+                tc_s(i + 2)
+            if ok(i + 2):
+                kn_s(i + 2)
 
         kv_sb = const.tile([P, B], F32)
         for h in range(2):

from contextlib import ExitStack

import concourse.mybir as mybir
from concourse.masks import make_identity

F32 = mybir.dt.float32
BF16 = mybir.dt.bfloat16
U32 = mybir.dt.uint32
U8 = mybir.dt.uint8
FP8X4 = mybir.dt.float8_e4m3fn_x4
ACT = mybir.ActivationFunctionType
ALU = mybir.AluOpType
AX = mybir.AxisListType

P = 128
B, N, E, C = 512, 16384, 512, 128
GK = 512
NG = N // GK
T = 4
VCH = 4
TILE_ORDER = (0, 1, 3, 2)

G_COLS = 272
V_COLS = 0
GRAM_T = 2
XN_V = 0
RS_T = 2
RS_LAST = 1
GRAM_0 = 1
KB_BUFS = 3
SQ_I = NG

FLOPS = 2 * N * B * E + 2 * N * B * C


def split(g):
    late = {NG - 1: (0, 256), NG - 2: (G_COLS, 0), NG - 3: (G_COLS, 128)}
    return late.get(g, (G_COLS, V_COLS))


def gram_tiles(g):
    return GRAM_T if g >= 1 else GRAM_0


def scalar_banks(g):
    return 1 if g < 3 else g % 2


def tile_varkeys_kernel(tc, x, keys, values, out):
    nc = tc.nc
    with ExitStack() as ctx:
        ctx.enter_context(tc.manual_schedule())
        const = ctx.enter_context(tc.tile_pool(name="const", bufs=1))
        kin = ctx.enter_context(tc.tile_pool(name="kin", bufs=6))
        kbp = ctx.enter_context(tc.tile_pool(name="kbp", bufs=KB_BUFS))
        w2 = ctx.enter_context(tc.tile_pool(name="w2", bufs=2))
        w3 = ctx.enter_context(tc.tile_pool(name="w3", bufs=3))
        w5 = ctx.enter_context(tc.tile_pool(name="w5", bufs=5))
        ps_t = ctx.enter_context(tc.psum_pool(name="ps_t", bufs=2))
        ps_s = ctx.enter_context(tc.psum_pool(name="ps_s", bufs=4))
        ps_g = ctx.enter_context(tc.psum_pool(name="ps_g", bufs=1))
        ps_kv = ctx.enter_context(tc.psum_pool(name="ps_kv", bufs=1))

        keys_g = keys.rearrange("(g p t) e -> g p t e", p=P, t=T)
        vals_g = values.rearrange("(g p t) c -> p g t c", p=P, t=T)
        st = {}

        def ok(g):
            return 0 <= g < NG

        def load_keys(g):
            k_sb = kin.tile([P, T, E], BF16, name="k_sb")
            nc.sync.dma_start(out=k_sb[:], in_=keys_g[g])
            st[("k", g)] = k_sb

        v_sb = const.tile([P, NG, T, C], BF16)

        def load_values(j):
            nc.sync.dma_start(out=v_sb[:, VCH * j : VCH * (j + 1)], in_=vals_g[:, VCH * j : VCH * (j + 1)])

        one = const.tile([P, 1], F32)
        nc.vector.memset(one[:], 1.0)
        warm = const.tile([P, 1], F32)
        nc.scalar.activation(out=warm[:], in_=one[:], func=ACT.Abs_reciprocal_sqrt)
        ident = const.tile([P, P], F32)
        make_identity(nc, ident[:])

        x_sb = const.tile([P, 4, E], BF16)
        x_v = x.rearrange("(bt p) e -> p bt e", p=P)
        for bt in range(4):
            nc.sync.dma_start(out=x_sb[:, bt, :], in_=x_v[:, bt, :])
        load_keys(0)
        load_keys(1)
        load_keys(2)
        load_values(0)

        x_m2 = const.tile([P, 4, E], BF16)
        for bt in range(4):
            nc.vector.tensor_scalar_mul(out=x_m2[:, bt, :], in0=x_sb[:, bt, :], scalar1=-2.0)

        junk = const.tile([P, E], BF16)
        xn = const.tile([P, 4], F32)
        junk_v = const.tile([P, E], F32)
        for bt in range(4):
            if bt < XN_V:
                nc.vector.scalar_tensor_tensor(
                    out=junk_v[:],
                    in0=x_sb[:, bt, :],
                    scalar=1.0,
                    in1=x_sb[:, bt, :],
                    op0=ALU.mult,
                    op1=ALU.mult,
                    accum_out=xn[:, bt : bt + 1],
                )
            else:
                nc.scalar.activation(out=junk[:], in_=x_sb[:, bt, :], func=ACT.Square, accum_out=xn[:, bt : bt + 1])

        def transposes(src, pool, tag):
            banks = []
            for j in range(2):
                pt = pool.tile([P, 2, 2 * P], F32, name="pt", tag=tag)
                for tt in range(2):
                    words = src[:, 2 * j + tt, :].bitcast(F32)
                    for u in range(2):
                        nc.tensor.transpose(pt[:, u, P * tt : P * (tt + 1)], words[:, P * u : P * (u + 1)], ident[:])
                banks.append(pt)
            return banks

        def copy_out(banks, grouped, j, on_scalar):
            dst = grouped[:].bitcast(F32).rearrange("p (k u) -> p k u", u=2)[:, 2 * P * j : 2 * P * (j + 1), :]
            src = banks[j][:].rearrange("p u k -> p k u")
            if on_scalar:
                nc.scalar.copy(out=dst, in_=src)
            else:
                nc.vector.tensor_copy(out=dst, in_=src)

        xg = const.tile([P, 4 * B], BF16, align_bytes=64)
        x_banks = transposes(x_m2, ps_s, "s")
        st[("pt", 0)] = transposes(st[("k", 0)], ps_t, "pt")
        copy_out(x_banks, xg, 0, False)
        copy_out(x_banks, xg, 1, False)
        xc = const.tile([P, B], U32, align_bytes=64)
        xs = const.tile([P, B], U8, align_bytes=64)
        xb1 = const.tile([P, B], F32)

        xb_ps = ps_s.tile([P, B], F32, name="xb_ps", tag="s")
        for bt in range(4):
            nc.tensor.transpose(xb_ps[:, P * bt : P * (bt + 1)], xn[:, bt : bt + 1].to_broadcast([P, P]), ident[:])

        vc = const.tile([P, NG * C], U32, align_bytes=64)
        vs = const.tile([P, NG * C], U8, align_bytes=64)
        kv_ps = ps_kv.tile([P, B], F32)

        nc.vector.quantize_mx(out=xc[:].bitcast(FP8X4), scales=xs[:], in_=xg[:])

        def val_copy(g):
            vg = w3.tile([P, C, T], BF16, name="vg", align_bytes=64)
            nc.gpsimd.tensor_scalar(
                out=vg[:],
                in0=v_sb[:, g].rearrange("p t c -> p c t"),
                scalar1=1.0,
                scalar2=0.0,
                op0=ALU.mult,
                op1=ALU.add,
            )
            st[("vg", g)] = vg

        def val_quant(g):
            cols = slice(C * g, C * (g + 1))
            nc.vector.quantize_mx(
                out=vc[:, cols].bitcast(FP8X4), scales=vs[:, cols], in_=st[("vg", g)][:].rearrange("p c t -> p (c t)")
            )

        def tr(g):
            st[("pt", g)] = transposes(st[("k", g)], ps_t, "pt")

        def tc_alloc(g):
            st[("kg", g)] = w3.tile([P, 4 * GK], BF16, name="kg", align_bytes=64)

        def tc_v(g):
            for j in range(2 - scalar_banks(g)):
                copy_out(st[("pt", g)], st[("kg", g)], j, False)

        def tc_s(g):
            for j in range(2 - scalar_banks(g), 2):
                copy_out(st[("pt", g)], st[("kg", g)], j, True)

        def kn_s(g):
            n_s = T - gram_tiles(g)
            kn = w5.tile([P, T], F32, name="kn")
            st[("kn", g)] = kn
            k_sb = st[("k", g)]
            for t in range(n_s):
                nc.scalar.activation(out=junk[:], in_=k_sb[:, t, :], func=ACT.Square, accum_out=kn[:, t : t + 1])

        def gram(g):
            n_g = gram_tiles(g)
            if n_g == 0:
                return
            kg3 = st[("kg", g)][:].rearrange("p (k j) -> p k j", j=4)
            gr = ps_g.tile([P, GRAM_T, P], F32, name="gr")
            for k in range(n_g):
                t = T - n_g + k
                for j in range(4):
                    a = kg3[:, P * t : P * (t + 1), j]
                    nc.tensor.matmul(out=gr[:, k, :], lhsT=a, rhs=a, start=(j == 0), stop=(j == 3))
            st[("gr", g)] = gr

        def diag(g):
            n_g = gram_tiles(g)
            if n_g == 0:
                return
            kng = w5.tile([P, GRAM_T], F32, name="kng")
            for k in range(n_g):
                dj = w2.tile([P, P], F32, name="dj")
                nc.vector.scalar_tensor_tensor(
                    out=dj[:],
                    in0=st[("gr", g)][:, k, :],
                    scalar=1.0,
                    in1=ident[:],
                    op0=ALU.mult,
                    op1=ALU.mult,
                    accum_out=kng[:, k : k + 1],
                )
            st[("kng", g)] = kng

        def qk(g):
            kc = w2.tile([P, GK], U32, name="kc", align_bytes=64)
            ks = w2.tile([P, GK], U8, name="ks", align_bytes=64)
            nc.vector.quantize_mx(out=kc[:].bitcast(FP8X4), scales=ks[:], in_=st[("kg", g)][:])
            st[("kc", g)] = (kc, ks)

        def m1(g, t):
            kc, ks = st[("kc", g)]
            s_ps = ps_s.tile([P, B], F32, name="s_ps", tag="s")
            cols = slice(P * t, P * (t + 1))
            nc.tensor.matmul_mx(
                out=s_ps[:],
                lhsT=kc[:, cols].bitcast(FP8X4),
                lhsT_scale=ks[:, cols],
                rhs=xc[:].bitcast(FP8X4),
                rhs_scale=xs[:],
                start=True,
                stop=True,
            )
            st[("s", g, t)] = s_ps

        def stt(g, t):
            if t == TILE_ORDER[0]:
                st[("y", g)] = w3.tile([P, T, B], F32, name="y")
            n_s = T - gram_tiles(g)
            if t < n_s:
                kn_t = st[("kn", g)][:, t : t + 1]
            else:
                kn_t = st[("kng", g)][:, t - n_s : t - n_s + 1]
            nc.vector.scalar_tensor_tensor(
                out=st[("y", g)][:, t, :], in0=st[("s", g, t)][:], scalar=kn_t, in1=xb1[:], op0=ALU.add, op1=ALU.add
            )

        def rs(g):
            st[("r", g)] = w3.tile([P, T, B], F32, name="r")
            step = RS_LAST if g == NG - 1 else RS_T
            for t in range(0, T, step):
                nc.scalar.activation(
                    out=st[("r", g)][:, t : t + step, :],
                    in_=st[("y", g)][:, t : t + step, :],
                    func=ACT.Abs_reciprocal_sqrt,
                )

        def sq_views(g, lo, hi, run):
            return (
                st[("kb", g)][:, lo:hi, :].rearrange("p (c i) t -> p c t i", i=run),
                st[("r", g)][:, :, lo:hi].rearrange("p t (c i) -> p c t i", i=run),
            )

        def sq_alloc(g):
            st[("kb", g)] = kbp.tile([P, B, T], BF16, name="kb", tag="kb", align_bytes=64)

        def sq_g(g):
            gc = split(g)[0]
            if gc == 0:
                return
            o, i = sq_views(g, 0, gc, 1)
            nc.gpsimd.tensor_tensor(out=o, in0=i, in1=i, op=ALU.mult)

        def sq_v(g):
            gc, vcols = split(g)
            if vcols == 0:
                return
            o, i = sq_views(g, gc, gc + vcols, 4)
            nc.vector.tensor_tensor(out=o, in0=i, in1=i, op=ALU.mult)

        def sq_s(g):
            gc, vcols = split(g)
            if gc + vcols >= B:
                return
            o, i = sq_views(g, gc + vcols, B, 2)
            nc.scalar.activation(out=o, in_=i, func=ACT.Square)

        def qp(g):
            qc = w2.tile([P, B], U32, name="qc", align_bytes=64)
            qs = w2.tile([P, B], U8, name="qs", align_bytes=64)
            st[("qc", g)] = (qc, qs)
            nc.vector.quantize_mx(
                out=qc[:].bitcast(FP8X4), scales=qs[:], in_=st[("kb", g)][:].rearrange("p b t -> p (b t)")
            )

        def m2(g):
            qc, qs = st[("qc", g)]
            cols = slice(C * g, C * (g + 1))
            nc.tensor.matmul_mx(
                out=kv_ps[:],
                lhsT=vc[:, cols].bitcast(FP8X4),
                lhsT_scale=vs[:, cols],
                rhs=qc[:].bitcast(FP8X4),
                rhs_scale=qs[:],
                start=(g == 0),
                stop=(g == NG - 1),
            )

        for i in range(-2, NG + 3):
            if ok(i + 5) and i + 5 > 2:
                load_keys(i + 5)
            if (i + 2) % VCH == 0 and (i + 2) // VCH + 1 < NG // VCH:
                load_values((i + 2) // VCH + 1)
            if ok(i + 1):
                gram(i + 1)
            if ok(i + 3):
                tr(i + 3)
            if ok(i + 1):
                qk(i + 1)
            if ok(i):
                val_quant(i)
            if ok(i - 3):
                qp(i - 3)
            if ok(i - 2):
                sq_alloc(i - 2)
                sq_v(i - 2)
                sq_g(i - 2)
            if ok(i + 1):
                val_copy(i + 1)
            if i == -1:
                nc.vector.tensor_scalar_add(out=xb1[:], in0=xb_ps[:], scalar1=1.0)
            if ok(i + 2):
                tc_alloc(i + 2)
                tc_v(i + 2)
            if ok(i + 1):
                for t in TILE_ORDER:
                    m1(i + 1, t)
            if ok(i - 3):
                m2(i - 3)
            if ok(i):
                for t in TILE_ORDER:
                    stt(i, t)
            if ok(i + 1):
                diag(i + 1)
            if ok(i - 2) and i >= SQ_I:
                sq_s(i - 2)
            if ok(i - 1):
                rs(i - 1)
            if ok(i - 2) and i < SQ_I:
                sq_s(i - 2)
            if ok(i + 2):
                tc_s(i + 2)
            if ok(i + 2):
                kn_s(i + 2)

        kv_sb = const.tile([P, B], F32)
        for h in range(2):
            cols = slice(2 * P * h, 2 * P * (h + 1))
            nc.scalar.copy(out=kv_sb[:, cols], in_=kv_ps[:, cols])
        rsum = const.tile([P, 4], F32)
        o_ps = []
        for h in range(2):
            o_half = ps_t.tile([P, 2, C], F32, name="o_half", tag="pt")
            for k in range(2):
                bt = 2 * h + k
                nc.tensor.transpose(o_half[:, k, :], kv_sb[:, P * bt : P * (bt + 1)], ident[:])
            nc.vector.tensor_reduce(out=rsum[:, 2 * h : 2 * (h + 1)], in_=o_half[:], axis=AX.X, op=ALU.add)
            o_ps.append(o_half)
        rinv = const.tile([P, 4], F32)
        nc.vector.reciprocal(out=rinv[:], in_=rsum[:])
        o_sb = const.tile([P, 4, C], F32)
        out_v = out.rearrange("(bt p) c -> p bt c", p=P)
        nc.vector.tensor_tensor(
            out=o_sb[:, 0:2, :], in0=o_ps[0][:], in1=rinv[:, 0:2].unsqueeze(2).to_broadcast([P, 2, C]), op=ALU.mult
        )
        nc.sync.dma_start(out=out_v[:, 0:2, :], in_=o_sb[:, 0:2, :])
        for k in range(2):
            nc.scalar.activation(
                out=o_sb[:, 2 + k, :], in_=o_ps[1][:, k, :], func=ACT.Copy, scale=rinv[:, 2 + k : 3 + k]
            )
        nc.scalar.dma_start(out=out_v[:, 2:4, :], in_=o_sb[:, 2:4, :])
